import numpy as np
import ml_dtypes


def mxq(x, axis, fmt="e4m3"):
    dtype, down = {"e4m3": (ml_dtypes.float8_e4m3fn, 7), "e5m2": (ml_dtypes.float8_e5m2, 14)}[fmt]
    v = np.moveaxis(np.asarray(x, np.float32).astype(ml_dtypes.bfloat16).astype(np.float64), axis, -1)
    blocks = v.reshape(v.shape[:-1] + (-1, 32))
    amax = np.abs(blocks).max(-1, keepdims=True)
    byte = np.maximum(np.where(amax > 0, np.frexp(amax)[1] - 1 + 127, 0) - down, 1)
    scale = np.exp2(byte - 127.0)
    codes = (blocks / scale).astype(np.float32).astype(dtype).astype(np.float64)
    return np.moveaxis((codes * scale).reshape(v.shape), -1, axis)


WIDE = False


def mx_kscale(k):
    if not WIDE:
        return np.ones(k)
    levels = np.array([10, -10, 5, -5, 0])
    if k % 512:
        return np.exp2(np.random.permutation(np.resize(levels, k // 32))).repeat(32)
    a = np.empty((k // 512, 16))
    for p in range(k // 512):
        a[p, :8] = np.random.permutation(np.resize(levels, 8))
        for g in range(8):
            far = levels[np.abs(levels - a[p, g]) >= 10]
            a[p, g + 8] = far[np.random.randint(len(far))]
    return np.exp2(a.ravel()).repeat(32)


BF16 = ml_dtypes.bfloat16


def bf(x):
    return np.asarray(x, np.float32).astype(BF16)


def f64(x):
    return np.asarray(x).astype(np.float64)


B, H, W, C, F, K, G, RR = 4, 64, 64, 512, 128, 3, 16, 4
KK = K * K
P = B * H * W


def setup_inputs():
    s = mx_kscale(C)
    return {"x": bf(np.random.standard_normal((B, H, W, C)) * s),
            "Wi": bf(np.random.standard_normal((C, F)) / np.sqrt(C) / s[:, None]),
            "bi": bf(np.random.standard_normal(F) * 0.3),
            "w_span": bf(np.random.standard_normal((B, H, W, KK * G)) * 0.7)}


def reference(x, Wi, bi, w_span):
    xi = ((mxq(f64(x).reshape(P, C), 1, "e4m3") @ mxq(f64(Wi), 0, "e4m3")) + f64(bi)).reshape(B, H, W, F)
    pad = (K - 1) // 2
    xp = np.pad(xi, ((0, 0), (pad, pad), (pad, pad), (0, 0)))
    patches = np.stack([xp[:, i:i + H, j:j + W, :] for i in range(K) for j in range(K)], axis=-2)
    patches = patches.reshape(B, H, W, G, F // G, KK)
    w = f64(w_span).reshape(B, H, W, G, KK)[:, :, :, :, None, :]
    return (w * patches).sum(-1).reshape(B, H, W, F)

@@ -1,0 +1,266 @@
+from contextlib import ExitStack
+
+import concourse.mybir as mybir
+from concourse.masks import make_identity
+
+F32 = mybir.dt.float32
+BF16 = mybir.dt.bfloat16
+U32 = mybir.dt.uint32
+U8 = mybir.dt.uint8
+FP8X4 = mybir.dt.float8_e4m3fn_x4
+ADD = mybir.AluOpType.add
+MULT = mybir.AluOpType.mult
+
+P = 128
+IMAGES, HEIGHT, WIDTH = 4, 64, 64
+C_IN = 512
+C_OUT = 128
+TAPS = 9
+GROUPS = 16
+GROUP_CH = C_OUT // GROUPS
+GROUP_LEN = GROUP_CH * TAPS
+FLAT = TAPS * C_OUT
+
+PAIRS = IMAGES // 2
+QUAD = 4
+QUADS_PER_PAIR = HEIGHT // QUAD
+STEPS = PAIRS * QUADS_PER_PAIR
+
+PAD = 8
+ROW_W = PAD + P
+ROWS = HEIGHT + 3
+
+BANK = 512
+BANK_TAPS = BANK // C_OUT
+BANK_STEP = 3 * C_OUT
+
+GP_CH = 72
+
+FLOPS = 2 * IMAGES * HEIGHT * WIDTH * C_OUT * (C_IN + TAPS)
+
+
+def tile_involution2d_pa_t_kernel(tc, x, Wi, bi, w_span, out):
+    nc = tc.nc
+    with ExitStack() as ctx:
+        const = ctx.enter_context(tc.tile_pool(name="const", bufs=1))
+        x_pool = ctx.enter_context(tc.tile_pool(name="x_pool", bufs=4))
+        w_pool = ctx.enter_context(tc.tile_pool(name="w_pool", bufs=5))
+        mx_pool = ctx.enter_context(tc.tile_pool(name="mx_pool", bufs=2))
+        prod_pool = ctx.enter_context(tc.tile_pool(name="prod_pool", bufs=3))
+        fold_pool = ctx.enter_context(tc.tile_pool(name="fold_pool", bufs=1))
+        out_pool = ctx.enter_context(tc.tile_pool(name="out_pool", bufs=3))
+        xt_psum = ctx.enter_context(tc.psum_pool(name="xt_psum", bufs=2))
+        xi_psum = ctx.enter_context(tc.psum_pool(name="xi_psum", bufs=1))
+        tap_psum = ctx.enter_context(tc.psum_pool(name="tap_psum", bufs=5))
+
+        x_tiles, w_tiles, grouped_tiles, code_tiles = {}, {}, {}, {}
+        prod_tiles, out_tiles, banks = {}, {}, {}
+
+        def place(step):
+            pair, quad = divmod(step, QUADS_PER_PAIR)
+            return pair, quad * QUAD
+
+        def load_x(step):
+            pair, row0 = place(step)
+            x_sb = x_pool.tile([P, QUAD, C_IN], BF16, name="x_sb")
+            for r in range(2):
+                nc.sync.dma_start(
+                    out=x_sb[r:P:2, :, :],
+                    in_=x[2 * pair + r, row0 : row0 + QUAD, :, :].rearrange("u v k -> v u k"),
+                )
+            x_tiles[step] = x_sb
+
+        def load_w(step):
+            pair, row0 = place(step)
+            w_sb = w_pool.tile([P, QUAD, GROUPS * TAPS], BF16, name="w_sb")
+            for r in range(2):
+                nc.sync.dma_start(
+                    out=w_sb[r:P:2, :, :],
+                    in_=w_span[2 * pair + r, row0 : row0 + QUAD, :, :].rearrange("u v q -> v u q"),
+                )
+            w_tiles[step] = w_sb
+
+        for step in range(3):
+            load_x(step)
+
+        ident = const.tile([P, P], F32, name="ident")
+        make_identity(nc, ident[:])
+
+        wi_raw = const.tile([P, 4, C_OUT], BF16, name="wi_raw")
+        nc.sync.dma_start(
+            out=wi_raw[:],
+            in_=Wi.rearrange("(q t) c -> q t c", t=4),
+        )
+        wi_grouped = const.tile([P, C_OUT, 4], BF16, name="wi_grouped", align_bytes=64)
+        nc.vector.tensor_copy(out=wi_grouped[:], in_=wi_raw[:].rearrange("q t c -> q c t"))
+        wi_codes = const.tile([P, C_OUT], U32, name="wi_codes", align_bytes=64)
+        wi_scales = const.tile([P, C_OUT], U8, name="wi_scales", align_bytes=64)
+        nc.vector.quantize_mx(
+            out=wi_codes[:].bitcast(FP8X4),
+            scales=wi_scales[:],
+            in_=wi_grouped[:].rearrange("q c t -> q (c t)"),
+        )
+
+        bias_bf = const.tile([P, 1], BF16, name="bias_bf")
+        with nc.allow_non_contiguous_dma(reason="one bias value to each partition, once"):
+            nc.sync.dma_start(out=bias_bf[:], in_=bi.rearrange("(c o) -> c o", o=1))
+        bias = const.tile([P, 1], F32, name="bias")
+        nc.vector.tensor_copy(out=bias[:], in_=bias_bf[:])
+
+        xi_pad = []
+        for pair in range(PAIRS):
+            xi_sb = const.tile([P, ROWS, ROW_W], F32, name="xi_pad%d" % pair)
+            nc.gpsimd.memset(xi_sb[:, :, 0:PAD], 0.0)
+            nc.gpsimd.memset(xi_sb[:, 0:1, PAD:ROW_W], 0.0)
+            nc.gpsimd.memset(xi_sb[:, HEIGHT + 1 : ROWS, PAD:ROW_W], 0.0)
+            xi_pad.append(xi_sb)
+
+        def transpose_x(step):
+            x_sb = x_tiles.pop(step)
+            grouped = mx_pool.tile([P, QUAD * P, 4], BF16, name="grouped", align_bytes=64)
+            words = (
+                grouped[:]
+                .rearrange("q n t -> q (n t)")
+                .bitcast(F32)
+                .rearrange("q (a u n h) -> q a u n h", a=2, u=2, h=2)
+            )
+            for a in range(2):
+                xt = xt_psum.tile([P, 2, 2, P], F32, name="xt")
+                for u in range(2):
+                    x_words = x_sb[:, 2 * a + u, :].bitcast(F32)
+                    for h in range(2):
+                        nc.tensor.transpose(
+                            out=xt[:, u, h, :],
+                            in_=x_words[:, h : 2 * P : 2],
+                            identity=ident[:],
+                        )
+                nc.scalar.copy(out=words[:, a], in_=xt[:].rearrange("q u h n -> q u n h"))
+            grouped_tiles[step] = grouped
+
+        def quantise_x(step):
+            grouped = grouped_tiles.pop(step)
+            codes = mx_pool.tile([P, QUAD * P], U32, name="codes", align_bytes=64)
+            scales = mx_pool.tile([P, QUAD * P], U8, name="scales", align_bytes=64)
+            nc.vector.quantize_mx(
+                out=codes[:].bitcast(FP8X4),
+                scales=scales[:],
+                in_=grouped[:].rearrange("q n t -> q (n t)"),
+            )
+            code_tiles[step] = (codes, scales)
+
+        def project(step):
+            pair, row0 = place(step)
+            codes, scales = code_tiles.pop(step)
+            xi_ps = xi_psum.tile([P, QUAD * P], F32, name="xi_ps")
+            nc.tensor.matmul_mx(
+                out=xi_ps[:],
+                lhsT=wi_codes[:].bitcast(FP8X4),
+                lhsT_scale=wi_scales[:],
+                rhs=codes[:].bitcast(FP8X4),
+                rhs_scale=scales[:],
+                start=True,
+                stop=True,
+            )
+            nc.scalar.activation(
+                out=xi_pad[pair][:, 1 + row0 : 1 + row0 + QUAD, PAD:ROW_W],
+                in_=xi_ps[:].rearrange("c (u n) -> c u n", u=QUAD),
+                func=mybir.ActivationFunctionType.Identity,
+                bias=bias[:, 0:1],
+                scale=1.0,
+            )
+
+        bank_order = [(pair, row) for pair in range(PAIRS) for row in range(-1, HEIGHT + 1)]
+
+        def build_bank(pair, row):
+            flat = xi_pad[pair][:].rearrange("c r n -> c (r n)")
+            bank = tap_psum.tile([P, BANK], F32, name="bank")
+            for s in range(BANK_TAPS):
+                first = (row + 1 + s // 3) * ROW_W + PAD + 2 * (s % 3 - 1)
+                nc.tensor.transpose(
+                    out=bank[:, s * C_OUT : (s + 1) * C_OUT],
+                    in_=flat[:, first : first + P],
+                    identity=ident[:],
+                )
+            banks[(pair, row)] = bank
+
+        def multiply(pair, row, w_row, prod_row):
+            for b in range(3):
+                g0 = min(BANK_STEP * (b - 1) + BANK, FLAT) // GROUP_LEN if b else 0
+                g1 = min(BANK_STEP * b + BANK, FLAT) // GROUP_LEN
+                first = GROUP_LEN * g0 - BANK_STEP * b
+                nc.vector.tensor_tensor(
+                    out=prod_row[:, GROUP_LEN * g0 : GROUP_LEN * g1].rearrange(
+                        "p (g j m) -> p g j m", j=GROUP_CH, m=TAPS
+                    ),
+                    in0=banks[(pair, row - 1 + b)][
+                        :, first : first + GROUP_LEN * (g1 - g0)
+                    ].rearrange("p (g j m) -> p g j m", j=GROUP_CH, m=TAPS),
+                    in1=w_row[:, TAPS * g0 : TAPS * g1]
+                    .rearrange("p (g m) -> p g m", m=TAPS)
+                    .unsqueeze(2)
+                    .to_broadcast([P, g1 - g0, GROUP_CH, TAPS]),
+                    op=MULT,
+                )
+            banks.pop((pair, row - 1))
+
+        def fold_on_gpsimd(step):
+            terms = prod_tiles[step][:].rearrange("p u (o m) -> p u o m", m=TAPS)[:, :, 0:GP_CH, :]
+            sum4 = fold_pool.tile([P, QUAD, GP_CH, 4], F32, name="sum4")
+            sum2 = fold_pool.tile([P, QUAD, GP_CH, 2], F32, name="sum2")
+            sum1 = fold_pool.tile([P, QUAD, GP_CH], F32, name="sum1")
+            nc.gpsimd.tensor_tensor(
+                out=sum4[:], in0=terms[:, :, :, 0:4], in1=terms[:, :, :, 4:8], op=ADD
+            )
+            nc.gpsimd.tensor_tensor(
+                out=sum2[:], in0=sum4[:, :, :, 0:2], in1=sum4[:, :, :, 2:4], op=ADD
+            )
+            nc.gpsimd.tensor_tensor(
+                out=sum1[:], in0=sum2[:, :, :, 0], in1=sum2[:, :, :, 1], op=ADD
+            )
+            nc.gpsimd.tensor_tensor(
+                out=out_tiles[step][:, :, 0:GP_CH], in0=sum1[:], in1=terms[:, :, :, 8], op=ADD
+            )
+
+        def fold_on_vector_and_store(step):
+            pair, row0 = place(step)
+            terms = prod_tiles.pop(step)[:].rearrange("p u (o m) -> p u o m", m=TAPS)
+            out_sb = out_tiles.pop(step)
+            nc.vector.tensor_reduce(
+                out=out_sb[:, :, GP_CH:C_OUT],
+                in_=terms[:, :, GP_CH:C_OUT, :],
+                axis=mybir.AxisListType.X,
+                op=ADD,
+            )
+            for r in range(2):
+                nc.sync.dma_start(
+                    out=out[2 * pair + r, row0 : row0 + QUAD, :, :].rearrange("u v o -> v u o"),
+                    in_=out_sb[r:P:2, :, :],
+                )
+
+        built = 0
+        for step in range(-3, STEPS):
+            if step + 3 < STEPS:
+                transpose_x(step + 3)
+            if 0 <= step + 6 < STEPS:
+                load_x(step + 6)
+            if 0 <= step + 2 < STEPS:
+                quantise_x(step + 2)
+                load_w(step + 2)
+            if 0 <= step + 1 < STEPS:
+                project(step + 1)
+            if step < 0:
+                continue
+            pair, row0 = place(step)
+            prod_tiles[step] = prod_pool.tile([P, QUAD, FLAT], F32, name="prod")
+            out_tiles[step] = out_pool.tile([P, QUAD, C_OUT], F32, name="out_sb")
+            w_sb = w_tiles.pop(step)
+            for u in range(QUAD):
+                wanted = bank_order.index((pair, row0 + u + 1)) + 1
+                while built <= min(wanted, len(bank_order) - 1):
+                    build_bank(*bank_order[built])
+                    built += 1
+                multiply(pair, row0 + u, w_sb[:, u, :], prod_tiles[step][:, u, :])
+                if u == 0 and step > 0:
+                    fold_on_vector_and_store(step - 1)
+            fold_on_gpsimd(step)
+        fold_on_vector_and_store(STEPS - 1)

@@ -8,7 +8,6 @@ BF16 = mybir.dt.bfloat16
 U32 = mybir.dt.uint32
 U8 = mybir.dt.uint8
 FP8X4 = mybir.dt.float8_e4m3fn_x4
-ADD = mybir.AluOpType.add
 MULT = mybir.AluOpType.mult
 
 P = 128
@@ -34,8 +33,6 @@ BANK = 512
 BANK_TAPS = BANK // C_OUT
 BANK_STEP = 3 * C_OUT
 
-GP_CH = 72
-
 FLOPS = 2 * IMAGES * HEIGHT * WIDTH * C_OUT * (C_IN + TAPS)
 
 
@@ -44,17 +41,18 @@ def tile_involution2d_pa_t_kernel(tc, x, Wi, bi, w_span, out):
     with ExitStack() as ctx:
         const = ctx.enter_context(tc.tile_pool(name="const", bufs=1))
         x_pool = ctx.enter_context(tc.tile_pool(name="x_pool", bufs=4))
-        w_pool = ctx.enter_context(tc.tile_pool(name="w_pool", bufs=5))
+        w_pool = ctx.enter_context(tc.tile_pool(name="w_pool", bufs=4))
         mx_pool = ctx.enter_context(tc.tile_pool(name="mx_pool", bufs=2))
-        prod_pool = ctx.enter_context(tc.tile_pool(name="prod_pool", bufs=3))
-        fold_pool = ctx.enter_context(tc.tile_pool(name="fold_pool", bufs=1))
+        prod_pool = ctx.enter_context(tc.tile_pool(name="prod_pool", bufs=5))
+        sum_pool = ctx.enter_context(tc.tile_pool(name="sum_pool", bufs=2))
         out_pool = ctx.enter_context(tc.tile_pool(name="out_pool", bufs=3))
-        xt_psum = ctx.enter_context(tc.psum_pool(name="xt_psum", bufs=2))
-        xi_psum = ctx.enter_context(tc.psum_pool(name="xi_psum", bufs=1))
         tap_psum = ctx.enter_context(tc.psum_pool(name="tap_psum", bufs=5))
+        xt_psum = ctx.enter_context(tc.psum_pool(name="xt_psum", bufs=1))
+        sum_psum = ctx.enter_context(tc.psum_pool(name="sum_psum", bufs=1))
+        misc_psum = ctx.enter_context(tc.psum_pool(name="misc_psum", bufs=1))
 
         x_tiles, w_tiles, grouped_tiles, code_tiles = {}, {}, {}, {}
-        prod_tiles, out_tiles, banks = {}, {}, {}
+        prod_tiles, sum_banks, sum_tiles, out_tiles, banks = {}, {}, {}, {}, {}
 
         def place(step):
             pair, quad = divmod(step, QUADS_PER_PAIR)
@@ -80,62 +78,29 @@ def tile_involution2d_pa_t_kernel(tc, x, Wi, bi, w_span, out):
                 )
             w_tiles[step] = w_sb
 
-        for step in range(3):
-            load_x(step)
-
-        ident = const.tile([P, P], F32, name="ident")
-        make_identity(nc, ident[:])
-
-        wi_raw = const.tile([P, 4, C_OUT], BF16, name="wi_raw")
-        nc.sync.dma_start(
-            out=wi_raw[:],
-            in_=Wi.rearrange("(q t) c -> q t c", t=4),
-        )
-        wi_grouped = const.tile([P, C_OUT, 4], BF16, name="wi_grouped", align_bytes=64)
-        nc.vector.tensor_copy(out=wi_grouped[:], in_=wi_raw[:].rearrange("q t c -> q c t"))
-        wi_codes = const.tile([P, C_OUT], U32, name="wi_codes", align_bytes=64)
-        wi_scales = const.tile([P, C_OUT], U8, name="wi_scales", align_bytes=64)
-        nc.vector.quantize_mx(
-            out=wi_codes[:].bitcast(FP8X4),
-            scales=wi_scales[:],
-            in_=wi_grouped[:].rearrange("q c t -> q (c t)"),
-        )
-
-        bias_bf = const.tile([P, 1], BF16, name="bias_bf")
-        with nc.allow_non_contiguous_dma(reason="one bias value to each partition, once"):
-            nc.sync.dma_start(out=bias_bf[:], in_=bi.rearrange("(c o) -> c o", o=1))
-        bias = const.tile([P, 1], F32, name="bias")
-        nc.vector.tensor_copy(out=bias[:], in_=bias_bf[:])
-
-        xi_pad = []
-        for pair in range(PAIRS):
-            xi_sb = const.tile([P, ROWS, ROW_W], F32, name="xi_pad%d" % pair)
-            nc.gpsimd.memset(xi_sb[:, :, 0:PAD], 0.0)
-            nc.gpsimd.memset(xi_sb[:, 0:1, PAD:ROW_W], 0.0)
-            nc.gpsimd.memset(xi_sb[:, HEIGHT + 1 : ROWS, PAD:ROW_W], 0.0)
-            xi_pad.append(xi_sb)
-
-        def transpose_x(step):
-            x_sb = x_tiles.pop(step)
-            grouped = mx_pool.tile([P, QUAD * P, 4], BF16, name="grouped", align_bytes=64)
+        def transpose_x(step, half):
+            if half == 0:
+                grouped_tiles[step] = mx_pool.tile(
+                    [P, QUAD * P, 4], BF16, name="grouped", align_bytes=64
+                )
             words = (
-                grouped[:]
+                grouped_tiles[step][:]
                 .rearrange("q n t -> q (n t)")
                 .bitcast(F32)
                 .rearrange("q (a u n h) -> q a u n h", a=2, u=2, h=2)
             )
-            for a in range(2):
-                xt = xt_psum.tile([P, 2, 2, P], F32, name="xt")
-                for u in range(2):
-                    x_words = x_sb[:, 2 * a + u, :].bitcast(F32)
-                    for h in range(2):
-                        nc.tensor.transpose(
-                            out=xt[:, u, h, :],
-                            in_=x_words[:, h : 2 * P : 2],
-                            identity=ident[:],
-                        )
-                nc.scalar.copy(out=words[:, a], in_=xt[:].rearrange("q u h n -> q u n h"))
-            grouped_tiles[step] = grouped
+            xt = xt_psum.tile([P, 2, 2, P], F32, name="xt")
+            for u in range(2):
+                x_words = x_tiles[step][:, 2 * half + u, :].bitcast(F32)
+                for h in range(2):
+                    nc.tensor.transpose(
+                        out=xt[:, u, h, :],
+                        in_=x_words[:, h : 2 * P : 2],
+                        identity=ident[:],
+                    )
+            nc.scalar.copy(out=words[:, half], in_=xt[:].rearrange("q u h n -> q u n h"))
+            if half == 1:
+                x_tiles.pop(step)
 
         def quantise_x(step):
             grouped = grouped_tiles.pop(step)
@@ -151,7 +116,7 @@ def tile_involution2d_pa_t_kernel(tc, x, Wi, bi, w_span, out):
         def project(step):
             pair, row0 = place(step)
             codes, scales = code_tiles.pop(step)
-            xi_ps = xi_psum.tile([P, QUAD * P], F32, name="xi_ps")
+            xi_ps = misc_psum.tile([P, BANK], F32, name="misc")
             nc.tensor.matmul_mx(
                 out=xi_ps[:],
                 lhsT=wi_codes[:].bitcast(FP8X4),
@@ -183,84 +148,145 @@ def tile_involution2d_pa_t_kernel(tc, x, Wi, bi, w_span, out):
                 )
             banks[(pair, row)] = bank
 
-        def multiply(pair, row, w_row, prod_row):
+        def multiply(pair, row, w_row):
+            prod = prod_pool.tile([P, TAPS, C_OUT], F32, name="prod")
             for b in range(3):
                 g0 = min(BANK_STEP * (b - 1) + BANK, FLAT) // GROUP_LEN if b else 0
                 g1 = min(BANK_STEP * b + BANK, FLAT) // GROUP_LEN
                 first = GROUP_LEN * g0 - BANK_STEP * b
                 nc.vector.tensor_tensor(
-                    out=prod_row[:, GROUP_LEN * g0 : GROUP_LEN * g1].rearrange(
-                        "p (g j m) -> p g j m", j=GROUP_CH, m=TAPS
+                    out=prod[:, :, GROUP_CH * g0 : GROUP_CH * g1].rearrange(
+                        "p m (g j) -> p m g j", j=GROUP_CH
                     ),
                     in0=banks[(pair, row - 1 + b)][
                         :, first : first + GROUP_LEN * (g1 - g0)
-                    ].rearrange("p (g j m) -> p g j m", j=GROUP_CH, m=TAPS),
+                    ].rearrange("p (g j m) -> p m g j", j=GROUP_CH, m=TAPS),
                     in1=w_row[:, TAPS * g0 : TAPS * g1]
-                    .rearrange("p (g m) -> p g m", m=TAPS)
-                    .unsqueeze(2)
-                    .to_broadcast([P, g1 - g0, GROUP_CH, TAPS]),
+                    .rearrange("p (g m) -> p m g", m=TAPS)
+                    .unsqueeze(3)
+                    .to_broadcast([P, TAPS, g1 - g0, GROUP_CH]),
                     op=MULT,
                 )
             banks.pop((pair, row - 1))
+            return prod
 
-        def fold_on_gpsimd(step):
-            terms = prod_tiles[step][:].rearrange("p u (o m) -> p u o m", m=TAPS)[:, :, 0:GP_CH, :]
-            sum4 = fold_pool.tile([P, QUAD, GP_CH, 4], F32, name="sum4")
-            sum2 = fold_pool.tile([P, QUAD, GP_CH, 2], F32, name="sum2")
-            sum1 = fold_pool.tile([P, QUAD, GP_CH], F32, name="sum1")
-            nc.gpsimd.tensor_tensor(
-                out=sum4[:], in0=terms[:, :, :, 0:4], in1=terms[:, :, :, 4:8], op=ADD
-            )
-            nc.gpsimd.tensor_tensor(
-                out=sum2[:], in0=sum4[:, :, :, 0:2], in1=sum4[:, :, :, 2:4], op=ADD
-            )
-            nc.gpsimd.tensor_tensor(
-                out=sum1[:], in0=sum2[:, :, :, 0], in1=sum2[:, :, :, 1], op=ADD
-            )
-            nc.gpsimd.tensor_tensor(
-                out=out_tiles[step][:, :, 0:GP_CH], in0=sum1[:], in1=terms[:, :, :, 8], op=ADD
-            )
+        def add_up(step, u):
+            if u == 0:
+                sum_banks[step] = sum_psum.tile([P, BANK], F32, name="sums")
+            prod = prod_tiles.pop((step, u))
+            for m in range(TAPS):
+                nc.tensor.matmul(
+                    out=sum_banks[step][:, u * P : (u + 1) * P],
+                    lhsT=prod[:, m, :],
+                    rhs=ident[:],
+                    is_transpose=True,
+                    start=(m == 0),
+                    stop=(m == TAPS - 1),
+                )
+            if u == QUAD - 1:
+                sums_sb = sum_pool.tile([P, BANK], F32, name="sums_sb")
+                nc.scalar.copy(out=sums_sb[:], in_=sum_banks.pop(step)[:])
+                sum_tiles[step] = sums_sb
 
-        def fold_on_vector_and_store(step):
+        def turn_back(step):
+            sums_sb = sum_tiles.pop(step)
+            back = misc_psum.tile([P, BANK], F32, name="misc")
+            for u in range(QUAD):
+                nc.tensor.transpose(
+                    out=back[:, u * C_OUT : (u + 1) * C_OUT],
+                    in_=sums_sb[:, u * P : (u + 1) * P],
+                    identity=ident[:],
+                )
+            out_sb = out_pool.tile([P, QUAD, C_OUT], F32, name="out_sb")
+            nc.scalar.copy(out=out_sb[:].rearrange("p u o -> p (u o)"), in_=back[:])
+            out_tiles[step] = out_sb
+
+        def store(step):
             pair, row0 = place(step)
-            terms = prod_tiles.pop(step)[:].rearrange("p u (o m) -> p u o m", m=TAPS)
             out_sb = out_tiles.pop(step)
-            nc.vector.tensor_reduce(
-                out=out_sb[:, :, GP_CH:C_OUT],
-                in_=terms[:, :, GP_CH:C_OUT, :],
-                axis=mybir.AxisListType.X,
-                op=ADD,
-            )
             for r in range(2):
                 nc.sync.dma_start(
                     out=out[2 * pair + r, row0 : row0 + QUAD, :, :].rearrange("u v o -> v u o"),
                     in_=out_sb[r:P:2, :, :],
                 )
 
+        ctx.enter_context(tc.manual_schedule())
+        load_x(0)
+        wi_raw = const.tile([P, 4, C_OUT], BF16, name="wi_raw")
+        nc.sync.dma_start(out=wi_raw[:], in_=Wi.rearrange("(q t) c -> q t c", t=4))
+        bias_bf = const.tile([P, 1], BF16, name="bias_bf")
+        with nc.allow_non_contiguous_dma(reason="one bias value to each partition, once"):
+            nc.sync.dma_start(out=bias_bf[:], in_=bi.rearrange("(c o) -> c o", o=1))
+        load_x(1)
+        load_w(0)
+        load_x(2)
+        load_x(3)
+        load_w(1)
+
+        ident = const.tile([P, P], F32, name="ident")
+        make_identity(nc, ident[:])
+        xi_pad = []
+        for pair in range(PAIRS):
+            xi_sb = const.tile([P, ROWS, ROW_W], F32, name="xi_pad%d" % pair)
+            nc.gpsimd.memset(xi_sb[:, :, 0:PAD], 0.0)
+            nc.gpsimd.memset(xi_sb[:, 0:1, PAD:ROW_W], 0.0)
+            nc.gpsimd.memset(xi_sb[:, HEIGHT + 1 : ROWS, PAD:ROW_W], 0.0)
+            xi_pad.append(xi_sb)
+
+        wi_grouped = const.tile([P, C_OUT, 4], BF16, name="wi_grouped", align_bytes=64)
+        nc.vector.tensor_copy(out=wi_grouped[:], in_=wi_raw[:].rearrange("q t c -> q c t"))
+        bias = const.tile([P, 1], F32, name="bias")
+        nc.vector.tensor_copy(out=bias[:], in_=bias_bf[:])
+        wi_codes = const.tile([P, C_OUT], U32, name="wi_codes", align_bytes=64)
+        wi_scales = const.tile([P, C_OUT], U8, name="wi_scales", align_bytes=64)
+        nc.vector.quantize_mx(
+            out=wi_codes[:].bitcast(FP8X4),
+            scales=wi_scales[:],
+            in_=wi_grouped[:].rearrange("q c t -> q (c t)"),
+        )
+
         built = 0
-        for step in range(-3, STEPS):
-            if step + 3 < STEPS:
-                transpose_x(step + 3)
-            if 0 <= step + 6 < STEPS:
-                load_x(step + 6)
-            if 0 <= step + 2 < STEPS:
-                quantise_x(step + 2)
-                load_w(step + 2)
-            if 0 <= step + 1 < STEPS:
-                project(step + 1)
-            if step < 0:
-                continue
+
+        def build_until(wanted):
+            for i in range(built, min(wanted, len(bank_order) - 1) + 1):
+                build_bank(*bank_order[i])
+            return max(built, min(wanted, len(bank_order) - 1) + 1)
+
+        for half in range(2):
+            transpose_x(0, half)
+        quantise_x(0)
+        for half in range(2):
+            transpose_x(1, half)
+        quantise_x(1)
+        project(0)
+        built = build_until(2)
+        project(1)
+        for half in range(2):
+            transpose_x(2, half)
+
+        for step in range(STEPS):
             pair, row0 = place(step)
-            prod_tiles[step] = prod_pool.tile([P, QUAD, FLAT], F32, name="prod")
-            out_tiles[step] = out_pool.tile([P, QUAD, C_OUT], F32, name="out_sb")
             w_sb = w_tiles.pop(step)
+            if step >= 2:
+                store(step - 2)
+            if step + 4 < STEPS:
+                load_x(step + 4)
+            if step + 2 < STEPS:
+                load_w(step + 2)
             for u in range(QUAD):
-                wanted = bank_order.index((pair, row0 + u + 1)) + 1
-                while built <= min(wanted, len(bank_order) - 1):
-                    build_bank(*bank_order[built])
-                    built += 1
-                multiply(pair, row0 + u, w_sb[:, u, :], prod_tiles[step][:, u, :])
-                if u == 0 and step > 0:
-                    fold_on_vector_and_store(step - 1)
-            fold_on_gpsimd(step)
-        fold_on_vector_and_store(STEPS - 1)
+                if step + u > 0:
+                    add_up(*divmod(QUAD * step + u - 1, QUAD))
+                built = build_until(bank_order.index((pair, row0 + u + 1)) + 1)
+                prod_tiles[(step, u)] = multiply(pair, row0 + u, w_sb[:, u, :])
+                if u < 2 and step + 3 < STEPS:
+                    transpose_x(step + 3, u)
+                if u == 0 and step + 2 < STEPS:
+                    quantise_x(step + 2)
+                if u == 2 and step + 2 < STEPS:
+                    project(step + 2)
+                if u == 3 and step > 0:
+                    turn_back(step - 1)
+        store(STEPS - 2)
+        add_up(STEPS - 1, QUAD - 1)
+        turn_back(STEPS - 1)
+        store(STEPS - 1)

@@ -8,6 +8,7 @@ BF16 = mybir.dt.bfloat16
 U32 = mybir.dt.uint32
 U8 = mybir.dt.uint8
 FP8X4 = mybir.dt.float8_e4m3fn_x4
+ADD = mybir.AluOpType.add
 MULT = mybir.AluOpType.mult
 
 P = 128
@@ -44,6 +45,7 @@ def tile_involution2d_pa_t_kernel(tc, x, Wi, bi, w_span, out):
         w_pool = ctx.enter_context(tc.tile_pool(name="w_pool", bufs=4))
         mx_pool = ctx.enter_context(tc.tile_pool(name="mx_pool", bufs=2))
         prod_pool = ctx.enter_context(tc.tile_pool(name="prod_pool", bufs=5))
+        pair_pool = ctx.enter_context(tc.tile_pool(name="pair_pool", bufs=3))
         sum_pool = ctx.enter_context(tc.tile_pool(name="sum_pool", bufs=2))
         out_pool = ctx.enter_context(tc.tile_pool(name="out_pool", bufs=3))
         tap_psum = ctx.enter_context(tc.psum_pool(name="tap_psum", bufs=5))
@@ -52,6 +54,7 @@ def tile_involution2d_pa_t_kernel(tc, x, Wi, bi, w_span, out):
         misc_psum = ctx.enter_context(tc.psum_pool(name="misc_psum", bufs=1))
 
         x_tiles, w_tiles, grouped_tiles, code_tiles = {}, {}, {}, {}
+        pair_tiles = {}
         prod_tiles, sum_banks, sum_tiles, out_tiles, banks = {}, {}, {}, {}, {}
 
         def place(step):
@@ -170,18 +173,28 @@ def tile_involution2d_pa_t_kernel(tc, x, Wi, bi, w_span, out):
             banks.pop((pair, row - 1))
             return prod
 
+        def add_pairs(step, u):
+            prod = prod_tiles[(step, u)]
+            pairs = pair_pool.tile([P, 4, C_OUT], F32, name="pairs")
+            nc.gpsimd.tensor_tensor(
+                out=pairs[:], in0=prod[:, 0:4, :], in1=prod[:, 4:8, :], op=ADD
+            )
+            pair_tiles[(step, u)] = pairs
+
         def add_up(step, u):
             if u == 0:
                 sum_banks[step] = sum_psum.tile([P, BANK], F32, name="sums")
             prod = prod_tiles.pop((step, u))
-            for m in range(TAPS):
+            pairs = pair_tiles.pop((step, u))
+            parts = [pairs[:, m, :] for m in range(4)] + [prod[:, TAPS - 1, :]]
+            for m in range(5):
                 nc.tensor.matmul(
                     out=sum_banks[step][:, u * P : (u + 1) * P],
-                    lhsT=prod[:, m, :],
+                    lhsT=parts[m],
                     rhs=ident[:],
                     is_transpose=True,
                     start=(m == 0),
-                    stop=(m == TAPS - 1),
+                    stop=(m == 4),
                 )
             if u == QUAD - 1:
                 sums_sb = sum_pool.tile([P, BANK], F32, name="sums_sb")
@@ -274,19 +287,21 @@ def tile_involution2d_pa_t_kernel(tc, x, Wi, bi, w_span, out):
             if step + 2 < STEPS:
                 load_w(step + 2)
             for u in range(QUAD):
-                if step + u > 0:
-                    add_up(*divmod(QUAD * step + u - 1, QUAD))
+                if QUAD * step + u > 1:
+                    add_up(*divmod(QUAD * step + u - 2, QUAD))
                 built = build_until(bank_order.index((pair, row0 + u + 1)) + 1)
                 prod_tiles[(step, u)] = multiply(pair, row0 + u, w_sb[:, u, :])
+                add_pairs(step, u)
                 if u < 2 and step + 3 < STEPS:
                     transpose_x(step + 3, u)
                 if u == 0 and step + 2 < STEPS:
                     quantise_x(step + 2)
-                if u == 2 and step + 2 < STEPS:
+                if u == 3 and step + 2 < STEPS:
                     project(step + 2)
-                if u == 3 and step > 0:
+                if u == 2 and step > 0:
                     turn_back(step - 1)
         store(STEPS - 2)
+        add_up(STEPS - 1, QUAD - 2)
         add_up(STEPS - 1, QUAD - 1)
         turn_back(STEPS - 1)
         store(STEPS - 1)

@@ -43,7 +43,7 @@ def tile_involution2d_pa_t_kernel(tc, x, Wi, bi, w_span, out):
         const = ctx.enter_context(tc.tile_pool(name="const", bufs=1))
         x_pool = ctx.enter_context(tc.tile_pool(name="x_pool", bufs=4))
         w_pool = ctx.enter_context(tc.tile_pool(name="w_pool", bufs=4))
-        mx_pool = ctx.enter_context(tc.tile_pool(name="mx_pool", bufs=2))
+        mx_pool = ctx.enter_context(tc.tile_pool(name="mx_pool", bufs=3))
         prod_pool = ctx.enter_context(tc.tile_pool(name="prod_pool", bufs=5))
         pair_pool = ctx.enter_context(tc.tile_pool(name="pair_pool", bufs=3))
         sum_pool = ctx.enter_context(tc.tile_pool(name="sum_pool", bufs=2))
@@ -118,7 +118,7 @@ def tile_involution2d_pa_t_kernel(tc, x, Wi, bi, w_span, out):
 
         def project(step):
             pair, row0 = place(step)
-            codes, scales = code_tiles.pop(step)
+            codes, scales = code_tiles[step]
             xi_ps = misc_psum.tile([P, BANK], F32, name="misc")
             nc.tensor.matmul_mx(
                 out=xi_ps[:],
@@ -139,9 +139,20 @@ def tile_involution2d_pa_t_kernel(tc, x, Wi, bi, w_span, out):
 
         bank_order = [(pair, row) for pair in range(PAIRS) for row in range(-1, HEIGHT + 1)]
 
-        def build_bank(pair, row):
+        def build_bank(pair, row, warm=None):
             flat = xi_pad[pair][:].rearrange("c r n -> c (r n)")
             bank = tap_psum.tile([P, BANK], F32, name="bank")
+            if warm is not None:
+                codes, scales = code_tiles[warm]
+                nc.tensor.matmul_mx(
+                    out=bank[:],
+                    lhsT=wi_codes[:].bitcast(FP8X4),
+                    lhsT_scale=wi_scales[:],
+                    rhs=codes[:].bitcast(FP8X4),
+                    rhs_scale=scales[:],
+                    start=True,
+                    stop=True,
+                )
             for s in range(BANK_TAPS):
                 first = (row + 1 + s // 3) * ROW_W + PAD + 2 * (s % 3 - 1)
                 nc.tensor.transpose(
@@ -260,9 +271,9 @@ def tile_involution2d_pa_t_kernel(tc, x, Wi, bi, w_span, out):
 
         built = 0
 
-        def build_until(wanted):
+        def build_until(wanted, warm=None):
             for i in range(built, min(wanted, len(bank_order) - 1) + 1):
-                build_bank(*bank_order[i])
+                build_bank(*bank_order[i], warm=warm)
             return max(built, min(wanted, len(bank_order) - 1) + 1)
 
         for half in range(2):
@@ -289,7 +300,10 @@ def tile_involution2d_pa_t_kernel(tc, x, Wi, bi, w_span, out):
             for u in range(QUAD):
                 if QUAD * step + u > 1:
                     add_up(*divmod(QUAD * step + u - 2, QUAD))
-                built = build_until(bank_order.index((pair, row0 + u + 1)) + 1)
+                built = build_until(
+                    bank_order.index((pair, row0 + u + 1)) + 1,
+                    warm=min(step + 1, STEPS - 1) if u in (1, 2) else None,
+                )
                 prod_tiles[(step, u)] = multiply(pair, row0 + u, w_sb[:, u, :])
                 add_pairs(step, u)
                 if u < 2 and step + 3 < STEPS:

from contextlib import ExitStack

import concourse.mybir as mybir
from concourse.masks import make_identity

F32 = mybir.dt.float32
BF16 = mybir.dt.bfloat16
U32 = mybir.dt.uint32
U8 = mybir.dt.uint8
FP8X4 = mybir.dt.float8_e4m3fn_x4
ADD = mybir.AluOpType.add
MULT = mybir.AluOpType.mult

P = 128
IMAGES, HEIGHT, WIDTH = 4, 64, 64
C_IN = 512
C_OUT = 128
TAPS = 9
GROUPS = 16
GROUP_CH = C_OUT // GROUPS
GROUP_LEN = GROUP_CH * TAPS
FLAT = TAPS * C_OUT

PAIRS = IMAGES // 2
QUAD = 4
QUADS_PER_PAIR = HEIGHT // QUAD
STEPS = PAIRS * QUADS_PER_PAIR

PAD = 8
ROW_W = PAD + P
ROWS = HEIGHT + 3

BANK = 512
BANK_TAPS = BANK // C_OUT
BANK_STEP = 3 * C_OUT

FLOPS = 2 * IMAGES * HEIGHT * WIDTH * C_OUT * (C_IN + TAPS)


def tile_involution2d_pa_t_kernel(tc, x, Wi, bi, w_span, out):
    nc = tc.nc
    with ExitStack() as ctx:
        const = ctx.enter_context(tc.tile_pool(name="const", bufs=1))
        x_pool = ctx.enter_context(tc.tile_pool(name="x_pool", bufs=4))
        w_pool = ctx.enter_context(tc.tile_pool(name="w_pool", bufs=4))
        mx_pool = ctx.enter_context(tc.tile_pool(name="mx_pool", bufs=3))
        prod_pool = ctx.enter_context(tc.tile_pool(name="prod_pool", bufs=5))
        pair_pool = ctx.enter_context(tc.tile_pool(name="pair_pool", bufs=3))
        sum_pool = ctx.enter_context(tc.tile_pool(name="sum_pool", bufs=2))
        out_pool = ctx.enter_context(tc.tile_pool(name="out_pool", bufs=3))
        tap_psum = ctx.enter_context(tc.psum_pool(name="tap_psum", bufs=5))
        xt_psum = ctx.enter_context(tc.psum_pool(name="xt_psum", bufs=1))
        sum_psum = ctx.enter_context(tc.psum_pool(name="sum_psum", bufs=1))
        misc_psum = ctx.enter_context(tc.psum_pool(name="misc_psum", bufs=1))

        x_tiles, w_tiles, grouped_tiles, code_tiles = {}, {}, {}, {}
        pair_tiles = {}
        prod_tiles, sum_banks, sum_tiles, out_tiles, banks = {}, {}, {}, {}, {}

        def place(step):
            pair, quad = divmod(step, QUADS_PER_PAIR)
            return pair, quad * QUAD

        def load_x(step):
            pair, row0 = place(step)
            x_sb = x_pool.tile([P, QUAD, C_IN], BF16, name="x_sb")
            for r in range(2):
                nc.sync.dma_start(
                    out=x_sb[r:P:2, :, :],
                    in_=x[2 * pair + r, row0 : row0 + QUAD, :, :].rearrange("u v k -> v u k"),
                )
            x_tiles[step] = x_sb

        def load_w(step):
            pair, row0 = place(step)
            w_sb = w_pool.tile([P, QUAD, GROUPS * TAPS], BF16, name="w_sb")
            for r in range(2):
                nc.sync.dma_start(
                    out=w_sb[r:P:2, :, :],
                    in_=w_span[2 * pair + r, row0 : row0 + QUAD, :, :].rearrange("u v q -> v u q"),
                )
            w_tiles[step] = w_sb

        def transpose_x(step, half):
            if half == 0:
                grouped_tiles[step] = mx_pool.tile(
                    [P, QUAD * P, 4], BF16, name="grouped", align_bytes=64
                )
            words = (
                grouped_tiles[step][:]
                .rearrange("q n t -> q (n t)")
                .bitcast(F32)
                .rearrange("q (a u n h) -> q a u n h", a=2, u=2, h=2)
            )
            xt = xt_psum.tile([P, 2, 2, P], F32, name="xt")
            for u in range(2):
                x_words = x_tiles[step][:, 2 * half + u, :].bitcast(F32)
                for h in range(2):
                    nc.tensor.transpose(
                        out=xt[:, u, h, :],
                        in_=x_words[:, h : 2 * P : 2],
                        identity=ident[:],
                    )
            nc.scalar.copy(out=words[:, half], in_=xt[:].rearrange("q u h n -> q u n h"))
            if half == 1:
                x_tiles.pop(step)

        def quantise_x(step):
            grouped = grouped_tiles.pop(step)
            codes = mx_pool.tile([P, QUAD * P], U32, name="codes", align_bytes=64)
            scales = mx_pool.tile([P, QUAD * P], U8, name="scales", align_bytes=64)
            nc.vector.quantize_mx(
                out=codes[:].bitcast(FP8X4),
                scales=scales[:],
                in_=grouped[:].rearrange("q n t -> q (n t)"),
            )
            code_tiles[step] = (codes, scales)

        def project(step):
            pair, row0 = place(step)
            codes, scales = code_tiles[step]
            xi_ps = misc_psum.tile([P, BANK], F32, name="misc")
            nc.tensor.matmul_mx(
                out=xi_ps[:],
                lhsT=wi_codes[:].bitcast(FP8X4),
                lhsT_scale=wi_scales[:],
                rhs=codes[:].bitcast(FP8X4),
                rhs_scale=scales[:],
                start=True,
                stop=True,
            )
            nc.scalar.activation(
                out=xi_pad[pair][:, 1 + row0 : 1 + row0 + QUAD, PAD:ROW_W],
                in_=xi_ps[:].rearrange("c (u n) -> c u n", u=QUAD),
                func=mybir.ActivationFunctionType.Identity,
                bias=bias[:, 0:1],
                scale=1.0,
            )

        bank_order = [(pair, row) for pair in range(PAIRS) for row in range(-1, HEIGHT + 1)]

        def build_bank(pair, row, warm=None):
            flat = xi_pad[pair][:].rearrange("c r n -> c (r n)")
            bank = tap_psum.tile([P, BANK], F32, name="bank")
            if warm is not None:
                codes, scales = code_tiles[warm]
                nc.tensor.matmul_mx(
                    out=bank[:],
                    lhsT=wi_codes[:].bitcast(FP8X4),
                    lhsT_scale=wi_scales[:],
                    rhs=codes[:].bitcast(FP8X4),
                    rhs_scale=scales[:],
                    start=True,
                    stop=True,
                )
            for s in range(BANK_TAPS):
                first = (row + 1 + s // 3) * ROW_W + PAD + 2 * (s % 3 - 1)
                nc.tensor.transpose(
                    out=bank[:, s * C_OUT : (s + 1) * C_OUT],
                    in_=flat[:, first : first + P],
                    identity=ident[:],
                )
            banks[(pair, row)] = bank

        def multiply(pair, row, w_row):
            prod = prod_pool.tile([P, TAPS, C_OUT], F32, name="prod")
            for b in range(3):
                g0 = min(BANK_STEP * (b - 1) + BANK, FLAT) // GROUP_LEN if b else 0
                g1 = min(BANK_STEP * b + BANK, FLAT) // GROUP_LEN
                first = GROUP_LEN * g0 - BANK_STEP * b
                nc.vector.tensor_tensor(
                    out=prod[:, :, GROUP_CH * g0 : GROUP_CH * g1].rearrange(
                        "p m (g j) -> p m g j", j=GROUP_CH
                    ),
                    in0=banks[(pair, row - 1 + b)][
                        :, first : first + GROUP_LEN * (g1 - g0)
                    ].rearrange("p (g j m) -> p m g j", j=GROUP_CH, m=TAPS),
                    in1=w_row[:, TAPS * g0 : TAPS * g1]
                    .rearrange("p (g m) -> p m g", m=TAPS)
                    .unsqueeze(3)
                    .to_broadcast([P, TAPS, g1 - g0, GROUP_CH]),
                    op=MULT,
                )
            banks.pop((pair, row - 1))
            return prod

        def add_pairs(step, u):
            prod = prod_tiles[(step, u)]
            pairs = pair_pool.tile([P, 4, C_OUT], F32, name="pairs")
            nc.gpsimd.tensor_tensor(
                out=pairs[:], in0=prod[:, 0:4, :], in1=prod[:, 4:8, :], op=ADD
            )
            pair_tiles[(step, u)] = pairs

        def add_up(step, u):
            if u == 0:
                sum_banks[step] = sum_psum.tile([P, BANK], F32, name="sums")
            prod = prod_tiles.pop((step, u))
            pairs = pair_tiles.pop((step, u))
            parts = [pairs[:, m, :] for m in range(4)] + [prod[:, TAPS - 1, :]]
            for m in range(5):
                nc.tensor.matmul(
                    out=sum_banks[step][:, u * P : (u + 1) * P],
                    lhsT=parts[m],
                    rhs=ident[:],
                    is_transpose=True,
                    start=(m == 0),
                    stop=(m == 4),
                )
            if u == QUAD - 1:
                sums_sb = sum_pool.tile([P, BANK], F32, name="sums_sb")
                nc.scalar.copy(out=sums_sb[:], in_=sum_banks.pop(step)[:])
                sum_tiles[step] = sums_sb

        def turn_back(step):
            sums_sb = sum_tiles.pop(step)
            back = misc_psum.tile([P, BANK], F32, name="misc")
            for u in range(QUAD):
                nc.tensor.transpose(
                    out=back[:, u * C_OUT : (u + 1) * C_OUT],
                    in_=sums_sb[:, u * P : (u + 1) * P],
                    identity=ident[:],
                )
            out_sb = out_pool.tile([P, QUAD, C_OUT], F32, name="out_sb")
            nc.scalar.copy(out=out_sb[:].rearrange("p u o -> p (u o)"), in_=back[:])
            out_tiles[step] = out_sb

        def store(step):
            pair, row0 = place(step)
            out_sb = out_tiles.pop(step)
            for r in range(2):
                nc.sync.dma_start(
                    out=out[2 * pair + r, row0 : row0 + QUAD, :, :].rearrange("u v o -> v u o"),
                    in_=out_sb[r:P:2, :, :],
                )

        ctx.enter_context(tc.manual_schedule())
        load_x(0)
        wi_raw = const.tile([P, 4, C_OUT], BF16, name="wi_raw")
        nc.sync.dma_start(out=wi_raw[:], in_=Wi.rearrange("(q t) c -> q t c", t=4))
        bias_bf = const.tile([P, 1], BF16, name="bias_bf")
        with nc.allow_non_contiguous_dma(reason="one bias value to each partition, once"):
            nc.sync.dma_start(out=bias_bf[:], in_=bi.rearrange("(c o) -> c o", o=1))
        load_x(1)
        load_w(0)
        load_x(2)
        load_x(3)
        load_w(1)

        ident = const.tile([P, P], F32, name="ident")
        make_identity(nc, ident[:])
        xi_pad = []
        for pair in range(PAIRS):
            xi_sb = const.tile([P, ROWS, ROW_W], F32, name="xi_pad%d" % pair)
            nc.gpsimd.memset(xi_sb[:, :, 0:PAD], 0.0)
            nc.gpsimd.memset(xi_sb[:, 0:1, PAD:ROW_W], 0.0)
            nc.gpsimd.memset(xi_sb[:, HEIGHT + 1 : ROWS, PAD:ROW_W], 0.0)
            xi_pad.append(xi_sb)

        wi_grouped = const.tile([P, C_OUT, 4], BF16, name="wi_grouped", align_bytes=64)
        nc.vector.tensor_copy(out=wi_grouped[:], in_=wi_raw[:].rearrange("q t c -> q c t"))
        bias = const.tile([P, 1], F32, name="bias")
        nc.vector.tensor_copy(out=bias[:], in_=bias_bf[:])
        wi_codes = const.tile([P, C_OUT], U32, name="wi_codes", align_bytes=64)
        wi_scales = const.tile([P, C_OUT], U8, name="wi_scales", align_bytes=64)
        nc.vector.quantize_mx(
            out=wi_codes[:].bitcast(FP8X4),
            scales=wi_scales[:],
            in_=wi_grouped[:].rearrange("q c t -> q (c t)"),
        )

        built = 0

        def build_until(wanted, warm=None):
            for i in range(built, min(wanted, len(bank_order) - 1) + 1):
                build_bank(*bank_order[i], warm=warm)
            return max(built, min(wanted, len(bank_order) - 1) + 1)

        for half in range(2):
            transpose_x(0, half)
        quantise_x(0)
        for half in range(2):
            transpose_x(1, half)
        quantise_x(1)
        project(0)
        built = build_until(2)
        project(1)
        for half in range(2):
            transpose_x(2, half)

        for step in range(STEPS):
            pair, row0 = place(step)
            w_sb = w_tiles.pop(step)
            if step >= 2:
                store(step - 2)
            if step + 4 < STEPS:
                load_x(step + 4)
            if step + 2 < STEPS:
                load_w(step + 2)
            for u in range(QUAD):
                if QUAD * step + u > 1:
                    add_up(*divmod(QUAD * step + u - 2, QUAD))
                built = build_until(
                    bank_order.index((pair, row0 + u + 1)) + 1,
                    warm=min(step + 1, STEPS - 1) if u in (1, 2) else None,
                )
                prod_tiles[(step, u)] = multiply(pair, row0 + u, w_sb[:, u, :])
                add_pairs(step, u)
                if u < 2 and step + 3 < STEPS:
                    transpose_x(step + 3, u)
                if u == 0 and step + 2 < STEPS:
                    quantise_x(step + 2)
                if u == 3 and step + 2 < STEPS:
                    project(step + 2)
                if u == 2 and step > 0:
                    turn_back(step - 1)
        store(STEPS - 2)
        add_up(STEPS - 1, QUAD - 2)
        add_up(STEPS - 1, QUAD - 1)
        turn_back(STEPS - 1)
        store(STEPS - 1)
